import numpy as np
import ml_dtypes


def mxq(x, axis, fmt="e4m3"):
    dtype, down = {"e4m3": (ml_dtypes.float8_e4m3fn, 7), "e5m2": (ml_dtypes.float8_e5m2, 14)}[fmt]
    v = np.moveaxis(np.asarray(x, np.float32).astype(ml_dtypes.bfloat16).astype(np.float64), axis, -1)
    blocks = v.reshape(v.shape[:-1] + (-1, 32))
    amax = np.abs(blocks).max(-1, keepdims=True)
    byte = np.maximum(np.where(amax > 0, np.frexp(amax)[1] - 1 + 127, 0) - down, 1)
    scale = np.exp2(byte - 127.0)
    codes = (blocks / scale).astype(np.float32).astype(dtype).astype(np.float64)
    return np.moveaxis((codes * scale).reshape(v.shape), -1, axis)


WIDE = False


def mx_kscale(k):
    if not WIDE:
        return np.ones(k)
    levels = np.array([10, -10, 5, -5, 0])
    if k % 512:
        return np.exp2(np.random.permutation(np.resize(levels, k // 32))).repeat(32)
    a = np.empty((k // 512, 16))
    for p in range(k // 512):
        a[p, :8] = np.random.permutation(np.resize(levels, 8))
        for g in range(8):
            far = levels[np.abs(levels - a[p, g]) >= 10]
            a[p, g + 8] = far[np.random.randint(len(far))]
    return np.exp2(a.ravel()).repeat(32)


BF16 = ml_dtypes.bfloat16


def bf(x):
    return np.asarray(x, np.float32).astype(BF16)


def f64(x):
    return np.asarray(x).astype(np.float64)


B, C, ROWS, COLS, H, W = 512, 16, 32, 32, 16, 32
K = ROWS * COLS
N = H * W
DENSITY = 0.1


def setup_inputs():
    s = mx_kscale(K)
    image = np.random.standard_normal((B, C, K)) * s
    votes = (np.random.random_sample((K, N)) < DENSITY) * (1.0 + 0.25 * np.random.standard_normal((K, N))) / s[:, None]
    return {"image": bf(image.reshape(B, C, ROWS, COLS)), "vote_index": bf(votes.reshape(ROWS, COLS, H, W))}


def reference(image, vote_index):
    rows, cols, h, w = vote_index.shape
    b, c = image.shape[0], image.shape[1]
    V = f64(vote_index).reshape(rows * cols, h * w)
    x = np.maximum(f64(image).reshape(b * c, rows * cols), 0.0)
    ht = (mxq(x, 1, "e4m3") @ mxq(V, 0, "e4m3")) / cols
    return ht.reshape(b, c, h, w)

@@ -1,0 +1,180 @@
+from contextlib import ExitStack
+
+import concourse.mybir as mybir
+from concourse.masks import make_identity
+
+BF16 = mybir.dt.bfloat16
+F32 = mybir.dt.float32
+U32 = mybir.dt.uint32
+U8 = mybir.dt.uint8
+FP8X4 = mybir.dt.float8_e4m3fn_x4
+COPY = mybir.ActivationFunctionType.Copy
+
+P = 128
+M = 8192
+K = 1024
+N = 512
+FLOPS = 2 * M * K * N
+
+MT = M // P
+GROUP = 4
+NG = MT // GROUP
+SLOT = 8
+LOADS = [2, 2, 4, 4, 4, 8, 8, 8, 8, 8, 8]
+STORES = [8, 8, 8, 8, 8, 4, 4, 4, 4, 4, 2, 2]
+
+
+def tile_ht_t_kernel(tc, image, vote_index, out):
+    nc = tc.nc
+    x_dram = image.rearrange("(p s) c r w -> p (s c r w)", s=4)
+    o_dram = out.rearrange("(p s) c h w -> p (s c h w)", s=4)
+    v_dram = vote_index.rearrange("r w h v -> (r w) (h v)").rearrange(
+        "(g q t) n -> q g (t n)", g=2, t=4
+    )
+    store_ends = {}
+    pos = 0
+    for cnt in STORES:
+        store_ends[pos + cnt] = pos
+        pos += cnt
+
+    with ExitStack() as ctx:
+        const = ctx.enter_context(tc.tile_pool(name="const", bufs=1))
+        io = ctx.enter_context(tc.tile_pool(name="io", bufs=1))
+        work = ctx.enter_context(tc.tile_pool(name="work", bufs=2))
+        tps = ctx.enter_context(tc.psum_pool(name="tps", bufs=1))
+        ops = ctx.enter_context(tc.psum_pool(name="ops", bufs=1))
+        ctx.enter_context(tc.manual_schedule())
+
+        ident = const.tile([P, P], F32, name="ident")
+        make_identity(nc, ident[:])
+
+        x_sb = []
+        for c in range(MT // SLOT):
+            x_sb.append(io.tile([P, SLOT * K], BF16, name="x%d" % c, tag="io%d" % c))
+        o_sb = {}
+        vraw = const.tile([P, 2, 4 * N], BF16, name="vraw")
+        vgrp = const.tile([P, 2, N, 4], BF16, name="vgrp", align_bytes=64)
+        vcodes = const.tile([P, 2 * N], U32, name="vcodes", align_bytes=64)
+        vscl = const.tile([P, 2 * N], U8, name="vscl", align_bytes=64)
+
+        nc.sync.dma_start(out=vraw[:], in_=v_dram)
+        pos = 0
+        for cnt in LOADS:
+            c = pos // SLOT
+            lo = (pos % SLOT) * K
+            nc.sync.dma_start(
+                out=x_sb[c][:, lo : lo + cnt * K],
+                in_=x_dram[:, pos * K : (pos + cnt) * K],
+            )
+            pos += cnt
+
+        def relu(m0, cnt):
+            c = m0 // SLOT
+            lo = (m0 % SLOT) * K
+            ap = x_sb[c][:, lo : lo + cnt * K]
+            nc.vector.tensor_scalar_max(out=ap, in0=ap, scalar1=0.0)
+
+        def v_regroup(g, eng_copy):
+            src = vraw[:, g].rearrange("q (t n) -> q t n", t=4)
+            eng_copy(
+                out=vgrp[:, g].rearrange("q (c i) t -> q c t i", i=4),
+                in_=src.rearrange("q t (c i) -> q c t i", i=4),
+            )
+
+        def v_quant(g):
+            nc.vector.quantize_mx(
+                out=vcodes[:, N * g : N * g + N].bitcast(FP8X4),
+                scales=vscl[:, N * g : N * g + N],
+                in_=vgrp[:, g].rearrange("q n t -> q (n t)"),
+            )
+
+        tbs = {}
+        grp = {}
+        cod = {}
+        obs = {}
+
+        def transposes(i):
+            for b in range(GROUP):
+                m = GROUP * i + b
+                tb = tps.tile([P, 4, P], F32, name="tb%d" % b, tag="tb%d" % b)
+                tbs[b] = tb
+                xw = x_sb[m // SLOT][:].bitcast(F32)
+                lo = (m % SLOT) * (K // 2)
+                for j in range(4):
+                    w0 = lo + 256 * (j // 2)
+                    nc.tensor.transpose(
+                        tb[:, j, :], xw[:, w0 + j % 2 : w0 + 256 : 2], ident[:]
+                    )
+
+        def exits_t(i, engines):
+            grouped = work.tile([P, GROUP * K], BF16, name="grouped", tag="grouped", align_bytes=64)
+            grp[i] = grouped
+            gw = grouped[:].bitcast(F32)
+            for b in range(GROUP):
+                dst = gw[:, 512 * b : 512 * b + 512].rearrange("p (g r u) -> p g r u", g=2, u=2)
+                src = tbs[b][:].rearrange("p (g u) r -> p g r u", u=2)
+                if engines[b] == "v":
+                    nc.vector.tensor_copy(out=dst, in_=src)
+                else:
+                    nc.scalar.copy(out=dst, in_=src)
+
+        def quant(i):
+            codes = work.tile([P, GROUP * 256], U32, name="codes", tag="codes", align_bytes=64)
+            scl = work.tile([P, GROUP * 256], U8, name="scl", tag="scl", align_bytes=64)
+            cod[i] = (codes, scl)
+            nc.vector.quantize_mx(out=codes[:].bitcast(FP8X4), scales=scl[:], in_=grp[i][:])
+
+        def mx(i):
+            codes, scl = cod[i]
+            for b in range(GROUP):
+                ob = ops.tile([P, N], F32, name="ob%d" % b, tag="ob%d" % b)
+                obs[b] = ob
+                for g in range(2):
+                    lo = 256 * b + P * g
+                    nc.tensor.matmul_mx(
+                        out=ob[:],
+                        lhsT=codes[:, lo : lo + P].bitcast(FP8X4),
+                        lhsT_scale=scl[:, lo : lo + P],
+                        rhs=vcodes[:, N * g : N * g + N].bitcast(FP8X4),
+                        rhs_scale=vscl[:, N * g : N * g + N],
+                        start=(g == 0),
+                        stop=(g == 1),
+                    )
+
+        def exits_o(i):
+            for b in range(GROUP):
+                m = GROUP * i + b
+                c = m // SLOT
+                if m % SLOT == 0:
+                    o_sb[c] = io.tile([P, SLOT * N], F32, name="o%d" % c, tag="io%d" % c)
+                lo = (m % SLOT) * N
+                nc.scalar.activation(
+                    out=o_sb[c][:, lo : lo + N], in_=obs[b][:], func=COPY, scale=1.0 / 32.0
+                )
+                if (m + 1) in store_ends:
+                    s0 = store_ends[m + 1]
+                    nc.sync.dma_start(
+                        out=o_dram[:, s0 * N : (m + 1) * N],
+                        in_=o_sb[c][:, (s0 % SLOT) * N : lo + N],
+                    )
+
+        v_regroup(0, nc.vector.tensor_copy)
+        v_regroup(1, nc.scalar.copy)
+        relu(0, 2)
+        v_quant(0)
+        relu(2, 2)
+        v_quant(1)
+        transposes(0)
+        exits_t(0, "ssss")
+        relu(4, 4)
+        quant(0)
+        for i in range(NG):
+            if i + 1 < NG:
+                transposes(i + 1)
+                exits_t(i + 1, "vsvs")
+            if i + 2 < NG:
+                relu(GROUP * (i + 2), GROUP)
+            if i + 1 < NG:
+                quant(i + 1)
+            mx(i)
+            exits_o(i)

@@ -29,7 +29,7 @@ def tile_ht_t_kernel(tc, image, vote_index, out):
     x_dram = image.rearrange("(p s) c r w -> p (s c r w)", s=4)
     o_dram = out.rearrange("(p s) c h w -> p (s c h w)", s=4)
     v_dram = vote_index.rearrange("r w h v -> (r w) (h v)").rearrange(
-        "(g q t) n -> q g (t n)", g=2, t=4
+        "(g b u w e) n -> g u b w (e n)", g=2, b=16, u=2, w=8, e=2
     )
     store_ends = {}
     pos = 0
@@ -40,13 +40,16 @@ def tile_ht_t_kernel(tc, image, vote_index, out):
     with ExitStack() as ctx:
         const = ctx.enter_context(tc.tile_pool(name="const", bufs=1))
         io = ctx.enter_context(tc.tile_pool(name="io", bufs=1))
-        work = ctx.enter_context(tc.tile_pool(name="work", bufs=2))
+        work = ctx.enter_context(tc.tile_pool(name="work", bufs=3))
         tps = ctx.enter_context(tc.psum_pool(name="tps", bufs=1))
         ops = ctx.enter_context(tc.psum_pool(name="ops", bufs=1))
         ctx.enter_context(tc.manual_schedule())
 
         ident = const.tile([P, P], F32, name="ident")
         make_identity(nc, ident[:])
+        warm = const.tile([P, 1], F32, name="warm")
+        nc.vector.memset(warm[:], 0.0)
+        nc.scalar.activation(out=warm[:], in_=warm[:], func=COPY)
 
         x_sb = []
         for c in range(MT // SLOT):
@@ -57,7 +60,11 @@ def tile_ht_t_kernel(tc, image, vote_index, out):
         vcodes = const.tile([P, 2 * N], U32, name="vcodes", align_bytes=64)
         vscl = const.tile([P, 2 * N], U8, name="vscl", align_bytes=64)
 
-        nc.sync.dma_start(out=vraw[:], in_=v_dram)
+        for g in range(2):
+            for u in range(2):
+                nc.sync.dma_start(
+                    out=vraw[:, g, 2 * N * u : 2 * N * (u + 1)], in_=v_dram[g, u]
+                )
         pos = 0
         for cnt in LOADS:
             c = pos // SLOT
@@ -68,11 +75,25 @@ def tile_ht_t_kernel(tc, image, vote_index, out):
             )
             pos += cnt
 
+        xps = {}
+
         def relu(m0, cnt):
             c = m0 // SLOT
             lo = (m0 % SLOT) * K
-            ap = x_sb[c][:, lo : lo + cnt * K]
-            nc.vector.tensor_scalar_max(out=ap, in0=ap, scalar1=0.0)
+            i = m0 // GROUP
+            if m0 % GROUP == 0:
+                xps[i] = work.tile([P, GROUP * K], BF16, name="xp", tag="xp", align_bytes=64)
+            po = (m0 % GROUP) * K
+            dst = xps[i][:, po : po + cnt * K].rearrange(
+                "p (h u b e) -> p h u b e", u=2, b=16, e=16
+            )
+            src = x_sb[c][:, lo : lo + cnt * K].rearrange(
+                "p (h b u e) -> p h b u e", u=2, b=16, e=16
+            )
+            for u in range(2):
+                nc.vector.tensor_scalar_max(
+                    out=dst[:, :, u], in0=src[:, :, :, u], scalar1=0.0
+                )
 
         def v_regroup(g, eng_copy):
             src = vraw[:, g].rearrange("q (t n) -> q t n", t=4)
@@ -98,12 +119,11 @@ def tile_ht_t_kernel(tc, image, vote_index, out):
                 m = GROUP * i + b
                 tb = tps.tile([P, 4, P], F32, name="tb%d" % b, tag="tb%d" % b)
                 tbs[b] = tb
-                xw = x_sb[m // SLOT][:].bitcast(F32)
-                lo = (m % SLOT) * (K // 2)
+                xw = xps[i][:].bitcast(F32)
+                lo = b * (K // 2)
                 for j in range(4):
-                    w0 = lo + 256 * (j // 2)
                     nc.tensor.transpose(
-                        tb[:, j, :], xw[:, w0 + j % 2 : w0 + 256 : 2], ident[:]
+                        tb[:, j, :], xw[:, lo + P * j : lo + P * j + P], ident[:]
                     )
 
         def exits_t(i, engines):

@@ -60,13 +60,14 @@ def tile_ht_t_kernel(tc, image, vote_index, out):
         vcodes = const.tile([P, 2 * N], U32, name="vcodes", align_bytes=64)
         vscl = const.tile([P, 2 * N], U8, name="vscl", align_bytes=64)
 
-        for g in range(2):
-            for u in range(2):
-                nc.sync.dma_start(
-                    out=vraw[:, g, 2 * N * u : 2 * N * (u + 1)], in_=v_dram[g, u]
-                )
         pos = 0
         for cnt in LOADS:
+            if pos == LOADS[0]:
+                for g in range(2):
+                    for u in range(2):
+                        nc.sync.dma_start(
+                            out=vraw[:, g, 2 * N * u : 2 * N * (u + 1)], in_=v_dram[g, u]
+                        )
             c = pos // SLOT
             lo = (pos % SLOT) * K
             nc.sync.dma_start(
@@ -95,11 +96,11 @@ def tile_ht_t_kernel(tc, image, vote_index, out):
                     out=dst[:, :, u], in0=src[:, :, :, u], scalar1=0.0
                 )
 
-        def v_regroup(g, eng_copy):
+        def v_regroup(g, eng_copy, lo=0, hi=N):
             src = vraw[:, g].rearrange("q (t n) -> q t n", t=4)
             eng_copy(
-                out=vgrp[:, g].rearrange("q (c i) t -> q c t i", i=4),
-                in_=src.rearrange("q t (c i) -> q c t i", i=4),
+                out=vgrp[:, g, lo:hi].rearrange("q (c i) t -> q c t i", i=4),
+                in_=src[:, :, lo:hi].rearrange("q t (c i) -> q c t i", i=4),
             )
 
         def v_quant(g):
@@ -114,8 +115,8 @@ def tile_ht_t_kernel(tc, image, vote_index, out):
         cod = {}
         obs = {}
 
-        def transposes(i):
-            for b in range(GROUP):
+        def transposes(i, bs=range(GROUP)):
+            for b in bs:
                 m = GROUP * i + b
                 tb = tps.tile([P, 4, P], F32, name="tb%d" % b, tag="tb%d" % b)
                 tbs[b] = tb
@@ -126,11 +127,11 @@ def tile_ht_t_kernel(tc, image, vote_index, out):
                         tb[:, j, :], xw[:, lo + P * j : lo + P * j + P], ident[:]
                     )
 
-        def exits_t(i, engines):
-            grouped = work.tile([P, GROUP * K], BF16, name="grouped", tag="grouped", align_bytes=64)
-            grp[i] = grouped
-            gw = grouped[:].bitcast(F32)
-            for b in range(GROUP):
+        def exits_t(i, engines, bs=range(GROUP)):
+            if 0 in bs:
+                grp[i] = work.tile([P, GROUP * K], BF16, name="grouped", tag="grouped", align_bytes=64)
+            gw = grp[i][:].bitcast(F32)
+            for b in bs:
                 dst = gw[:, 512 * b : 512 * b + 512].rearrange("p (g r u) -> p g r u", g=2, u=2)
                 src = tbs[b][:].rearrange("p (g u) r -> p g r u", u=2)
                 if engines[b] == "v":
@@ -138,15 +139,21 @@ def tile_ht_t_kernel(tc, image, vote_index, out):
                 else:
                     nc.scalar.copy(out=dst, in_=src)
 
-        def quant(i):
-            codes = work.tile([P, GROUP * 256], U32, name="codes", tag="codes", align_bytes=64)
-            scl = work.tile([P, GROUP * 256], U8, name="scl", tag="scl", align_bytes=64)
-            cod[i] = (codes, scl)
-            nc.vector.quantize_mx(out=codes[:].bitcast(FP8X4), scales=scl[:], in_=grp[i][:])
-
-        def mx(i):
+        def quant(i, b0=0, b1=GROUP):
+            if b0 == 0:
+                codes = work.tile([P, GROUP * 256], U32, name="codes", tag="codes", align_bytes=64)
+                scl = work.tile([P, GROUP * 256], U8, name="scl", tag="scl", align_bytes=64)
+                cod[i] = (codes, scl)
             codes, scl = cod[i]
-            for b in range(GROUP):
+            nc.vector.quantize_mx(
+                out=codes[:, 256 * b0 : 256 * b1].bitcast(FP8X4),
+                scales=scl[:, 256 * b0 : 256 * b1],
+                in_=grp[i][:, K * b0 : K * b1],
+            )
+
+        def mx(i, bs=range(GROUP)):
+            codes, scl = cod[i]
+            for b in bs:
                 ob = ops.tile([P, N], F32, name="ob%d" % b, tag="ob%d" % b)
                 obs[b] = ob
                 for g in range(2):
@@ -161,8 +168,8 @@ def tile_ht_t_kernel(tc, image, vote_index, out):
                         stop=(g == 1),
                     )
 
-        def exits_o(i):
-            for b in range(GROUP):
+        def exits_o(i, bs=range(GROUP)):
+            for b in bs:
                 m = GROUP * i + b
                 c = m // SLOT
                 if m % SLOT == 0:
@@ -178,16 +185,23 @@ def tile_ht_t_kernel(tc, image, vote_index, out):
                         in_=o_sb[c][:, (s0 % SLOT) * N : lo + N],
                     )
 
-        v_regroup(0, nc.vector.tensor_copy)
-        v_regroup(1, nc.scalar.copy)
         relu(0, 2)
+        transposes(0, (0, 1))
+        exits_t(0, "ssss", (0, 1))
+        v_regroup(0, nc.vector.tensor_copy)
+        v_regroup(1, nc.vector.tensor_copy, 0, N // 2)
+        v_regroup(1, nc.scalar.copy, N // 2, N)
         v_quant(0)
         relu(2, 2)
+        transposes(0, (2, 3))
+        exits_t(0, "ssss", (2, 3))
         v_quant(1)
-        transposes(0)
-        exits_t(0, "ssss")
-        relu(4, 4)
-        quant(0)
+        quant(0, 0, 2)
+        relu(4, 2)
+        relu(6, 2)
+        quant(0, 2, 4)
+        mx(0, (0, 1))
+        exits_o(0, (0, 1))
         for i in range(NG):
             if i + 1 < NG:
                 transposes(i + 1)
@@ -196,5 +210,6 @@ def tile_ht_t_kernel(tc, image, vote_index, out):
                 relu(GROUP * (i + 2), GROUP)
             if i + 1 < NG:
                 quant(i + 1)
-            mx(i)
-            exits_o(i)
+            bs = (2, 3) if i == 0 else range(GROUP)
+            mx(i, bs)
+            exits_o(i, bs)

@@ -19,9 +19,9 @@ FLOPS = 2 * M * K * N
 MT = M // P
 GROUP = 4
 NG = MT // GROUP
-SLOT = 8
-LOADS = [2, 2, 4, 4, 4, 8, 8, 8, 8, 8, 8]
-STORES = [8, 8, 8, 8, 8, 4, 4, 4, 4, 4, 2, 2]
+SLOT = 16
+LOADS = [2, 2, 4, 8, 16, 16, 16]
+STORES = [16, 16, 16, 8, 4, 2, 1, 1]
 
 
 def tile_ht_t_kernel(tc, image, vote_index, out):
@@ -40,7 +40,7 @@ def tile_ht_t_kernel(tc, image, vote_index, out):
     with ExitStack() as ctx:
         const = ctx.enter_context(tc.tile_pool(name="const", bufs=1))
         io = ctx.enter_context(tc.tile_pool(name="io", bufs=1))
-        work = ctx.enter_context(tc.tile_pool(name="work", bufs=3))
+        work = ctx.enter_context(tc.tile_pool(name="work", bufs=2))
         tps = ctx.enter_context(tc.psum_pool(name="tps", bufs=1))
         ops = ctx.enter_context(tc.psum_pool(name="ops", bufs=1))
         ctx.enter_context(tc.manual_schedule())
@@ -83,7 +83,7 @@ def tile_ht_t_kernel(tc, image, vote_index, out):
             lo = (m0 % SLOT) * K
             i = m0 // GROUP
             if m0 % GROUP == 0:
-                xps[i] = work.tile([P, GROUP * K], BF16, name="xp", tag="xp", align_bytes=64)
+                xps[i] = work.tile([P, GROUP * K], BF16, name="xp", tag="xp", align_bytes=64, bufs=3)
             po = (m0 % GROUP) * K
             dst = xps[i][:, po : po + cnt * K].rearrange(
                 "p (h u b e) -> p h u b e", u=2, b=16, e=16
@@ -173,7 +173,8 @@ def tile_ht_t_kernel(tc, image, vote_index, out):
                 m = GROUP * i + b
                 c = m // SLOT
                 if m % SLOT == 0:
-                    o_sb[c] = io.tile([P, SLOT * N], F32, name="o%d" % c, tag="io%d" % c)
+                    tag = "io%d" % (c - 1) if c else "spare"
+                    o_sb[c] = io.tile([P, SLOT * N], F32, name="o%d" % c, tag=tag)
                 lo = (m % SLOT) * N
                 nc.scalar.activation(
                     out=o_sb[c][:, lo : lo + N], in_=obs[b][:], func=COPY, scale=1.0 / 32.0

@@ -20,8 +20,8 @@ MT = M // P
 GROUP = 4
 NG = MT // GROUP
 SLOT = 16
-LOADS = [2, 2, 4, 8, 16, 16, 16]
-STORES = [16, 16, 16, 8, 4, 2, 1, 1]
+LOADS = [2, 2, 4, 4, 4, 8, 8, 16, 16]
+STORES = [16, 16, 8, 8, 4, 4, 4, 2, 1, 1]
 
 
 def tile_ht_t_kernel(tc, image, vote_index, out):

from contextlib import ExitStack

import concourse.mybir as mybir
from concourse.masks import make_identity

BF16 = mybir.dt.bfloat16
F32 = mybir.dt.float32
U32 = mybir.dt.uint32
U8 = mybir.dt.uint8
FP8X4 = mybir.dt.float8_e4m3fn_x4
COPY = mybir.ActivationFunctionType.Copy

P = 128
M = 8192
K = 1024
N = 512
FLOPS = 2 * M * K * N

MT = M // P
GROUP = 4
NG = MT // GROUP
SLOT = 16
LOADS = [2, 2, 4, 4, 4, 8, 8, 16, 16]
STORES = [16, 16, 8, 8, 4, 4, 4, 2, 1, 1]


def tile_ht_t_kernel(tc, image, vote_index, out):
    nc = tc.nc
    x_dram = image.rearrange("(p s) c r w -> p (s c r w)", s=4)
    o_dram = out.rearrange("(p s) c h w -> p (s c h w)", s=4)
    v_dram = vote_index.rearrange("r w h v -> (r w) (h v)").rearrange(
        "(g b u w e) n -> g u b w (e n)", g=2, b=16, u=2, w=8, e=2
    )
    store_ends = {}
    pos = 0
    for cnt in STORES:
        store_ends[pos + cnt] = pos
        pos += cnt

    with ExitStack() as ctx:
        const = ctx.enter_context(tc.tile_pool(name="const", bufs=1))
        io = ctx.enter_context(tc.tile_pool(name="io", bufs=1))
        work = ctx.enter_context(tc.tile_pool(name="work", bufs=2))
        tps = ctx.enter_context(tc.psum_pool(name="tps", bufs=1))
        ops = ctx.enter_context(tc.psum_pool(name="ops", bufs=1))
        ctx.enter_context(tc.manual_schedule())

        ident = const.tile([P, P], F32, name="ident")
        make_identity(nc, ident[:])
        warm = const.tile([P, 1], F32, name="warm")
        nc.vector.memset(warm[:], 0.0)
        nc.scalar.activation(out=warm[:], in_=warm[:], func=COPY)

        x_sb = []
        for c in range(MT // SLOT):
            x_sb.append(io.tile([P, SLOT * K], BF16, name="x%d" % c, tag="io%d" % c))
        o_sb = {}
        vraw = const.tile([P, 2, 4 * N], BF16, name="vraw")
        vgrp = const.tile([P, 2, N, 4], BF16, name="vgrp", align_bytes=64)
        vcodes = const.tile([P, 2 * N], U32, name="vcodes", align_bytes=64)
        vscl = const.tile([P, 2 * N], U8, name="vscl", align_bytes=64)

        pos = 0
        for cnt in LOADS:
            if pos == LOADS[0]:
                for g in range(2):
                    for u in range(2):
                        nc.sync.dma_start(
                            out=vraw[:, g, 2 * N * u : 2 * N * (u + 1)], in_=v_dram[g, u]
                        )
            c = pos // SLOT
            lo = (pos % SLOT) * K
            nc.sync.dma_start(
                out=x_sb[c][:, lo : lo + cnt * K],
                in_=x_dram[:, pos * K : (pos + cnt) * K],
            )
            pos += cnt

        xps = {}

        def relu(m0, cnt):
            c = m0 // SLOT
            lo = (m0 % SLOT) * K
            i = m0 // GROUP
            if m0 % GROUP == 0:
                xps[i] = work.tile([P, GROUP * K], BF16, name="xp", tag="xp", align_bytes=64, bufs=3)
            po = (m0 % GROUP) * K
            dst = xps[i][:, po : po + cnt * K].rearrange(
                "p (h u b e) -> p h u b e", u=2, b=16, e=16
            )
            src = x_sb[c][:, lo : lo + cnt * K].rearrange(
                "p (h b u e) -> p h b u e", u=2, b=16, e=16
            )
            for u in range(2):
                nc.vector.tensor_scalar_max(
                    out=dst[:, :, u], in0=src[:, :, :, u], scalar1=0.0
                )

        def v_regroup(g, eng_copy, lo=0, hi=N):
            src = vraw[:, g].rearrange("q (t n) -> q t n", t=4)
            eng_copy(
                out=vgrp[:, g, lo:hi].rearrange("q (c i) t -> q c t i", i=4),
                in_=src[:, :, lo:hi].rearrange("q t (c i) -> q c t i", i=4),
            )

        def v_quant(g):
            nc.vector.quantize_mx(
                out=vcodes[:, N * g : N * g + N].bitcast(FP8X4),
                scales=vscl[:, N * g : N * g + N],
                in_=vgrp[:, g].rearrange("q n t -> q (n t)"),
            )

        tbs = {}
        grp = {}
        cod = {}
        obs = {}

        def transposes(i, bs=range(GROUP)):
            for b in bs:
                m = GROUP * i + b
                tb = tps.tile([P, 4, P], F32, name="tb%d" % b, tag="tb%d" % b)
                tbs[b] = tb
                xw = xps[i][:].bitcast(F32)
                lo = b * (K // 2)
                for j in range(4):
                    nc.tensor.transpose(
                        tb[:, j, :], xw[:, lo + P * j : lo + P * j + P], ident[:]
                    )

        def exits_t(i, engines, bs=range(GROUP)):
            if 0 in bs:
                grp[i] = work.tile([P, GROUP * K], BF16, name="grouped", tag="grouped", align_bytes=64)
            gw = grp[i][:].bitcast(F32)
            for b in bs:
                dst = gw[:, 512 * b : 512 * b + 512].rearrange("p (g r u) -> p g r u", g=2, u=2)
                src = tbs[b][:].rearrange("p (g u) r -> p g r u", u=2)
                if engines[b] == "v":
                    nc.vector.tensor_copy(out=dst, in_=src)
                else:
                    nc.scalar.copy(out=dst, in_=src)

        def quant(i, b0=0, b1=GROUP):
            if b0 == 0:
                codes = work.tile([P, GROUP * 256], U32, name="codes", tag="codes", align_bytes=64)
                scl = work.tile([P, GROUP * 256], U8, name="scl", tag="scl", align_bytes=64)
                cod[i] = (codes, scl)
            codes, scl = cod[i]
            nc.vector.quantize_mx(
                out=codes[:, 256 * b0 : 256 * b1].bitcast(FP8X4),
                scales=scl[:, 256 * b0 : 256 * b1],
                in_=grp[i][:, K * b0 : K * b1],
            )

        def mx(i, bs=range(GROUP)):
            codes, scl = cod[i]
            for b in bs:
                ob = ops.tile([P, N], F32, name="ob%d" % b, tag="ob%d" % b)
                obs[b] = ob
                for g in range(2):
                    lo = 256 * b + P * g
                    nc.tensor.matmul_mx(
                        out=ob[:],
                        lhsT=codes[:, lo : lo + P].bitcast(FP8X4),
                        lhsT_scale=scl[:, lo : lo + P],
                        rhs=vcodes[:, N * g : N * g + N].bitcast(FP8X4),
                        rhs_scale=vscl[:, N * g : N * g + N],
                        start=(g == 0),
                        stop=(g == 1),
                    )

        def exits_o(i, bs=range(GROUP)):
            for b in bs:
                m = GROUP * i + b
                c = m // SLOT
                if m % SLOT == 0:
                    tag = "io%d" % (c - 1) if c else "spare"
                    o_sb[c] = io.tile([P, SLOT * N], F32, name="o%d" % c, tag=tag)
                lo = (m % SLOT) * N
                nc.scalar.activation(
                    out=o_sb[c][:, lo : lo + N], in_=obs[b][:], func=COPY, scale=1.0 / 32.0
                )
                if (m + 1) in store_ends:
                    s0 = store_ends[m + 1]
                    nc.sync.dma_start(
                        out=o_dram[:, s0 * N : (m + 1) * N],
                        in_=o_sb[c][:, (s0 % SLOT) * N : lo + N],
                    )

        relu(0, 2)
        transposes(0, (0, 1))
        exits_t(0, "ssss", (0, 1))
        v_regroup(0, nc.vector.tensor_copy)
        v_regroup(1, nc.vector.tensor_copy, 0, N // 2)
        v_regroup(1, nc.scalar.copy, N // 2, N)
        v_quant(0)
        relu(2, 2)
        transposes(0, (2, 3))
        exits_t(0, "ssss", (2, 3))
        v_quant(1)
        quant(0, 0, 2)
        relu(4, 2)
        relu(6, 2)
        quant(0, 2, 4)
        mx(0, (0, 1))
        exits_o(0, (0, 1))
        for i in range(NG):
            if i + 1 < NG:
                transposes(i + 1)
                exits_t(i + 1, "vsvs")
            if i + 2 < NG:
                relu(GROUP * (i + 2), GROUP)
            if i + 1 < NG:
                quant(i + 1)
            bs = (2, 3) if i == 0 else range(GROUP)
            mx(i, bs)
            exits_o(i, bs)
